import numpy as np
import ml_dtypes


def mxq(x, axis, fmt="e4m3"):
    dtype, down = {"e4m3": (ml_dtypes.float8_e4m3fn, 7), "e5m2": (ml_dtypes.float8_e5m2, 14)}[fmt]
    v = np.moveaxis(np.asarray(x, np.float32).astype(ml_dtypes.bfloat16).astype(np.float64), axis, -1)
    blocks = v.reshape(v.shape[:-1] + (-1, 32))
    amax = np.abs(blocks).max(-1, keepdims=True)
    byte = np.maximum(np.where(amax > 0, np.frexp(amax)[1] - 1 + 127, 0) - down, 1)
    scale = np.exp2(byte - 127.0)
    codes = (blocks / scale).astype(np.float32).astype(dtype).astype(np.float64)
    return np.moveaxis((codes * scale).reshape(v.shape), -1, axis)


WIDE = False


def mx_kscale(k):
    if not WIDE:
        return np.ones(k)
    levels = np.array([10, -10, 5, -5, 0])
    if k % 512:
        return np.exp2(np.random.permutation(np.resize(levels, k // 32))).repeat(32)
    a = np.empty((k // 512, 16))
    for p in range(k // 512):
        a[p, :8] = np.random.permutation(np.resize(levels, 8))
        for g in range(8):
            far = levels[np.abs(levels - a[p, g]) >= 10]
            a[p, g + 8] = far[np.random.randint(len(far))]
    return np.exp2(a.ravel()).repeat(32)


BF16 = ml_dtypes.bfloat16


def bf(x):
    return np.asarray(x, np.float32).astype(BF16)


def f64(x):
    return np.asarray(x).astype(np.float64)


B, K_SLOTS, P, SLOT, HID, NC, NP = 256, 8, 1536, 512, 512, 512, 512
KEY_SCALE = 3.0


def softmax(z):
    e = np.exp(z - z.max(-1, keepdims=True))
    return e / e.sum(-1, keepdims=True)


def draw0():
    rn = np.random.standard_normal
    s, t = mx_kscale(P), mx_kscale(P)
    return {"inst_embed": bf(rn((B, P)) * s),
            "Wfc": bf(rn((P, P)) / np.sqrt(P) / s[:, None] * t), "bfc": bf(0.3 * rn(P) * t),
            "Wfp": bf(rn((P, P)) / np.sqrt(P) / s[:, None] * t), "bfp": bf(0.3 * rn(P) * t),
            "Kc": bf(KEY_SCALE * rn((NC, P)) / t), "Kp": bf(KEY_SCALE * rn((NP, P)) / t)}


def core(inst_embed, Wfc, bfc, Wfp, bfp, Kc, Kp):
    xq = mxq(f64(inst_embed), 1, "e4m3")
    Qc = (xq @ mxq(f64(Wfc), 0, "e4m3")) + f64(bfc)
    Qp = (xq @ mxq(f64(Wfp), 0, "e4m3")) + f64(bfp)
    zc = (mxq(Qc, 1, "e4m3") @ mxq(f64(Kc), 1, "e4m3").T) / np.sqrt(P)
    zp = (mxq(Qp, 1, "e4m3") @ mxq(f64(Kp), 1, "e4m3").T) / np.sqrt(P)
    return softmax(zc), softmax(zp)


def e4m3fn_bytes(y):
    return np.clip(np.asarray(y, np.float64), -448.0, 448.0).astype(np.float32).astype(ml_dtypes.float8_e4m3fn).view(np.uint8)


def e4m3fn_values(b):
    return np.asarray(b, np.uint8).view(ml_dtypes.float8_e4m3fn).astype(np.float64)


def setup_inputs():
    d = draw0()
    x0 = np.asarray(d['Kp']).astype(np.float64)
    s = (np.max(np.abs(x0), axis=(0,), keepdims=True) / 448.0).astype(np.float32)
    out = {}
    for k, v in d.items():
        if k == 'Kp':
            out['Kp_bytes'] = e4m3fn_bytes(x0 / s.astype(np.float64))
            out['Kp_scale'] = s
        else:
            out[k] = v
    return out


def reference(inst_embed, Wfc, bfc, Wfp, bfp, Kc, Kp_bytes, Kp_scale):
    return core(inst_embed, Wfc, bfc, Wfp, bfp, Kc, e4m3fn_values(Kp_bytes) * Kp_scale.astype(np.float64))

@@ -1,0 +1,421 @@
+from contextlib import ExitStack
+
+import concourse.mybir as mybir
+from concourse.masks import make_identity
+
+F32 = mybir.dt.float32
+BF16 = mybir.dt.bfloat16
+U32 = mybir.dt.uint32
+U8 = mybir.dt.uint8
+FP8 = mybir.dt.float8_e4m3fn
+FP8X4 = mybir.dt.float8_e4m3fn_x4
+ALU = mybir.AluOpType
+ACT = mybir.ActivationFunctionType
+
+P = 128
+TOK = 256
+DIM = 1536
+KEYS = 512
+PASS = 512
+NPASS = DIM // PASS
+GROUP = 512
+NGROUP = DIM // GROUP
+SCALE = 1.0 / DIM ** 0.5
+FLOPS = 2 * TOK * DIM * DIM * 2 + 2 * TOK * KEYS * DIM * 2
+
+VQ = {(0, 1, 0): 1, (0, 1, 1): 0, (0, 2, 0): 4, (0, 2, 1): 2, (0, 1, 2): 4, (0, 2, 2): 0, (1, 0, 0): 0, (1, 1, 0): 0, (1, 2, 0): 0, (1, 0, 1): 4, (1, 1, 1): 4, (1, 2, 1): 2, (1, 0, 2): 1, (1, 1, 2): 0, (1, 2, 2): 0, (0, 0, 0): 4, (0, 0, 1): 0, (0, 0, 2): 0}
+LOADS = ("kp1", "002", "001", "kp0", "01*", "kc1", "x", "02*", "000", "kc0", "10*", "11*", "12*")
+ORDER = (
+    ("ilV", (0, 0, 2)),
+    ("sc", 0, "V"),
+    ("sc", 1, "S"),
+    ("ilV", (0, 0, 1)),
+    ("sc", 2, "V"),
+    ("ilS", (0, 0, 2)),
+    ("kt", 0, 0, 1),
+    ("pr", 2),
+    ("pr", 1),
+    ("pr", 3),
+    ("pr", 0),
+    ("ilS", (0, 0, 1)),
+    ("ilV", (0, 1, 2)),
+    ("ilS", (0, 1, 0)),
+    ("xt", 2),
+    ("xt", 1),
+    ("wq", (0, 0, 2)),
+    ("ilS", (0, 1, 1)),
+    ("ke", 0, 0, 1, "S"),
+    ("ilS", (0, 1, 2)),
+    ("xe", 2, "S"),
+    ("ilV", (0, 1, 0)),
+    ("wq", (0, 1, 2)),
+    ("xe", 1, "S"),
+    ("wq", (0, 0, 1)),
+    ("kt", 1, 1, 1),
+    ("xt", 0),
+    ("ke", 1, 1, 1, "S"),
+    ("ilS", (0, 2, 2)),
+    ("wq", (0, 1, 0)),
+    ("xe", 0, "S"),
+    ("kt", 1, 2, 0),
+    ("kt", 0, 1, 1),
+    ("ilV", (0, 1, 1)),
+    ("ke", 1, 2, 0, "S"),
+    ("ke", 0, 1, 1, "S"),
+    ("kt", 0, 0, 0),
+    ("wq", (0, 1, 1)),
+    ("kt", 0, 1, 0),
+    ("ilV", (0, 2, 2)),
+    ("ilS", (0, 2, 0)),
+    ("xq", 1),
+    ("ilV", (0, 2, 1)),
+    ("ilS", (0, 0, 0)),
+    ("ilV", (0, 2, 0)),
+    ("kt", 0, 2, 1),
+    ("ilV", (0, 0, 0)),
+    ("ke", 0, 0, 0, "S"),
+    ("ilS", (1, 0, 1)),
+    ("ilS", (0, 2, 1)),
+    ("wq", (0, 2, 0)),
+    ("xq", 0),
+    ("xq", 2),
+    ("wq", (0, 0, 0)),
+    ("kq", 0, 0),
+    ("kt", 0, 2, 0),
+    ("pj", 0, 0, 0),
+    ("wq", (0, 2, 2)),
+    ("wq", (0, 2, 1)),
+    ("ke", 0, 1, 0, "S"),
+    ("ilV", (1, 0, 1)),
+    ("pj", 0, 0, 1),
+    ("pj", 0, 1, 0),
+    ("ke", 0, 2, 1, "S"),
+    ("qe", 0, 0, 0),
+    ("kt", 1, 0, 1),
+    ("kt", 1, 0, 0),
+    ("ilV", (1, 0, 2)),
+    ("ilV", (1, 1, 0)),
+    ("qq", 0, 0, 0),
+    ("ke", 0, 2, 0, "S"),
+    ("kq", 0, 1),
+    ("ilS", (1, 0, 0)),
+    ("wq", (1, 0, 1)),
+    ("pj", 0, 1, 1),
+    ("qe", 0, 0, 1),
+    ("ilS", (1, 0, 2)),
+    ("ilV", (1, 1, 1)),
+    ("wq", (1, 0, 2)),
+    ("qq", 0, 0, 1),
+    ("scr", 0, 0, 0),
+    ("pj", 0, 2, 0),
+    ("ilS", (1, 1, 1)),
+    ("wq", (1, 1, 1)),
+    ("scr", 0, 0, 1),
+    ("kq", 0, 2),
+    ("kt", 1, 2, 1),
+    ("qe", 0, 1, 0),
+    ("ilV", (1, 2, 1)),
+    ("ke", 1, 0, 0, "S"),
+    ("ilV", (1, 0, 0)),
+    ("ilS", (1, 1, 0)),
+    ("pj", 0, 2, 1),
+    ("ilS", (1, 2, 1)),
+    ("qq", 0, 1, 0),
+    ("ilV", (1, 2, 0)),
+    ("qe", 0, 2, 0),
+    ("wq", (1, 0, 0)),
+    ("qe", 0, 1, 1),
+    ("wq", (1, 2, 1)),
+    ("scr", 0, 1, 0),
+    ("wq", (1, 1, 0)),
+    ("ke", 1, 0, 1, "S"),
+    ("qq", 0, 2, 0),
+    ("pj", 1, 1, 0),
+    ("pj", 1, 1, 1),
+    ("scr", 0, 2, 0),
+    ("ilS", (1, 2, 0)),
+    ("ilV", (1, 1, 2)),
+    ("ilS", (1, 2, 2)),
+    ("qq", 0, 1, 1),
+    ("ilV", (1, 2, 2)),
+    ("kq", 1, 0),
+    ("wq", (1, 2, 0)),
+    ("qe", 0, 2, 1),
+    ("pj", 1, 0, 1),
+    ("qe", 1, 1, 0),
+    ("pj", 1, 0, 0),
+    ("mx", 0, 0),
+    ("qe", 1, 1, 1),
+    ("qe", 1, 0, 1),
+    ("ilS", (1, 1, 2)),
+    ("qq", 1, 1, 0),
+    ("wq", (1, 2, 2)),
+    ("qq", 0, 2, 1),
+    ("qq", 1, 0, 1),
+    ("scr", 0, 1, 1),
+    ("qe", 1, 0, 0),
+    ("wq", (1, 1, 2)),
+    ("kt", 1, 1, 0),
+    ("scr", 0, 2, 1),
+    ("ke", 1, 2, 1, "S"),
+    ("mx", 0, 1),
+    ("pj", 1, 2, 0),
+    ("ex", 0, 0),
+    ("rc", 0, 0),
+    ("qq", 1, 0, 0),
+    ("kq", 1, 2),
+    ("pj", 1, 2, 1),
+    ("scr", 1, 0, 0),
+    ("qe", 1, 2, 0),
+    ("ke", 1, 1, 0, "S"),
+    ("kq", 1, 1),
+    ("qq", 1, 2, 0),
+    ("scr", 1, 1, 0),
+    ("ex", 0, 1),
+    ("scr", 1, 0, 1),
+    ("scr", 1, 2, 0),
+    ("qq", 1, 1, 1),
+    ("qe", 1, 2, 1),
+    ("nm", 0, 0),
+    ("scr", 1, 1, 1),
+    ("qq", 1, 2, 1),
+    ("scr", 1, 2, 1),
+    ("mx", 1, 0),
+    ("ex", 1, 0),
+    ("mx", 1, 1),
+    ("rc", 0, 1),
+    ("rc", 1, 0),
+    ("nm", 1, 0),
+    ("ex", 1, 1),
+    ("rc", 1, 1),
+    ("nm", 0, 1),
+    ("nm", 1, 1),
+)
+
+
+def tile_executor_pa_kernel(tc, inst_embed, Wfc, bfc, Wfp, bfp, Kc, Kp_bytes, Kp_scale, out_0, out_1):
+    nc = tc.nc
+    with ExitStack() as ctx:
+        keep = ctx.enter_context(tc.tile_pool(name="keep", bufs=1))
+        wpool = ctx.enter_context(tc.tile_pool(name="wpool", bufs=5))
+        stage = ctx.enter_context(tc.tile_pool(name="stage", bufs=3))
+        psum = ctx.enter_context(tc.psum_pool(name="psum", bufs=1))
+        ctx.enter_context(tc.manual_schedule())
+
+        scale_col = keep.tile([P, NPASS, 4], F32, name="scale_col", align_bytes=64)
+        nc.scalar.dma_start(out=scale_col[:], in_=Kp_scale.rearrange("o (g p t) -> p (o g) t", p=P, t=4))
+        ident = keep.tile([P, P], F32, name="ident", align_bytes=64)
+        make_identity(nc, ident[:])
+        warm = keep.tile([P, 1], F32, name="warm")
+        nc.vector.memset(warm[:], 0.0)
+        warm2 = keep.tile([P, 1], F32, name="warm2")
+        nc.scalar.activation(out=warm2[:], in_=warm[:], func=ACT.Exp)
+
+        W = (Wfc, Wfp)
+        wraw = {}
+        xraw = keep.tile([P, 2, DIM], BF16, name="xraw", align_bytes=64)
+        kpb = keep.tile([P, 4, DIM], U8, name="kpb", align_bytes=64)
+        kcr = keep.tile([P, 4, DIM], BF16, name="kcr", align_bytes=64)
+        biases = []
+        count = 0
+        for d in LOADS:
+            if d[0] == "k":
+                half = int(d[2])
+                if d[1] == "p":
+                    nc.sync.dma_start(out=kpb[:, 2 * half:2 * half + 2, :], in_=Kp_bytes.rearrange("(b p) k -> p b k", p=P)[:, 2 * half:2 * half + 2, :])
+                else:
+                    nc.sync.dma_start(out=kcr[:, 2 * half:2 * half + 2, :], in_=Kc.rearrange("(b p) k -> p b k", p=P)[:, 2 * half:2 * half + 2, :])
+            elif d == "x":
+                nc.sync.dma_start(out=xraw[:], in_=inst_embed.rearrange("(h p) k -> p h k", p=P))
+            else:
+                pr = int(d[0])
+                kp = int(d[1])
+                if (pr, kp) not in wraw:
+                    t = wpool.tile([P, 4, DIM], BF16, name="wraw", align_bytes=64)
+                    wraw[pr, kp] = t
+                t = wraw[pr, kp]
+                src = W[pr][kp * PASS:(kp + 1) * PASS, :].rearrange("(p j) n -> p j n", j=4)
+                if d[2] == "*":
+                    nc.sync.dma_start(out=t[:], in_=src)
+                else:
+                    g = int(d[2])
+                    nc.sync.dma_start(out=t[:, :, 512 * g:512 * g + 512], in_=src[:, :, 512 * g:512 * g + 512])
+            count += 1
+            if count == 6:
+                for i, b in enumerate((bfc, bfp)):
+                    bt = keep.tile([P, NGROUP, 4], BF16, name="bias%d" % i, align_bytes=64)
+                    nc.sync.dma_start(out=bt[:], in_=b.rearrange("(g p t) -> p g t", p=P, t=4))
+                    biases.append(bt)
+
+        wgrp = {}
+        wcodes = {}
+
+        def il_views(w):
+            if w not in wgrp:
+                wgrp[w] = stage.tile([P, 4 * GROUP], BF16, name="wgrp", bufs=5, align_bytes=64)
+            pr, kp, g = w
+            raw = wraw[pr, kp][:, :, g * GROUP:(g + 1) * GROUP]
+            d = wgrp[w][:].rearrange("p (t m j) -> p t m j", t=4, j=4)
+            s = raw.rearrange("p j (m t) -> p t m j", t=4)
+            return d, s
+
+        def ilS(w):
+            d, s = il_views(w)
+            cut = 4 - VQ[w]
+            if cut:
+                nc.scalar.copy(out=d[:, 0:cut], in_=s[:, 0:cut])
+
+        def ilV(w):
+            d, s = il_views(w)
+            cut = 4 - VQ[w]
+            if cut < 4:
+                nc.vector.tensor_copy(out=d[:, cut:4], in_=s[:, cut:4])
+
+        def wq(w):
+            codes = stage.tile([P, GROUP], U32, name="wcodes", bufs=13, align_bytes=64)
+            scales = stage.tile([P, GROUP], U8, name="wscales", bufs=13, align_bytes=64)
+            nc.vector.quantize_mx(out=codes[:].bitcast(FP8X4), scales=scales[:], in_=wgrp[w][:])
+            wcodes[w] = (codes, scales)
+
+        def copy(e, out, in_):
+            if e == "S":
+                nc.scalar.copy(out=out, in_=in_)
+            else:
+                nc.vector.tensor_copy(out=out, in_=in_)
+
+        xcodes = {}
+        xbank = {}
+        xgrp = keep.tile([P, NPASS, 4 * TOK], BF16, name="xgrp", align_bytes=64)
+
+        def xt(g):
+            bank = psum.tile([P, 2, 2, P], F32, name="tbank", bufs=3)
+            for h in range(2):
+                words = xraw[:, h, :].bitcast(F32)
+                for u in range(2):
+                    nc.tensor.transpose(bank[:, h, u, :], words[:, 256 * g + u:256 * (g + 1):2], ident[:])
+            xbank[g] = bank
+
+        def xe(g, e):
+            copy(e, xgrp[:, g, :].bitcast(F32).rearrange("p (h r u) -> p h r u", h=2, u=2),
+                 xbank[g][:].rearrange("p h u r -> p h r u"))
+
+        def xq(g):
+            codes = keep.tile([P, TOK], U32, name="xcodes%d" % g, align_bytes=64)
+            scales = keep.tile([P, TOK], U8, name="xscales%d" % g, align_bytes=64)
+            nc.vector.quantize_mx(out=codes[:].bitcast(FP8X4), scales=scales[:], in_=xgrp[:, g, :])
+            xcodes[g] = (codes, scales)
+
+        scale_b = keep.tile([P, DIM], F32, name="scale_b", align_bytes=64)
+
+        def sc(g, e):
+            bank = psum.tile([P, 4, P], F32, name="tbank", bufs=3)
+            for t in range(4):
+                nc.tensor.transpose(bank[:, t, :], scale_col[:, g, t:t + 1].to_broadcast([P, P]), ident[:])
+            copy(e, scale_b[:, g * PASS:(g + 1) * PASS].rearrange("p (n t) -> p n t", t=4),
+                 bank[:].rearrange("p t n -> p n t"))
+
+        kpr = keep.tile([P, 4, DIM], BF16, name="kpr", align_bytes=64)
+
+        def pr(b):
+            nc.vector.tensor_tensor(out=kpr[:, b, :], in0=kpb[:, b, :].bitcast(FP8), in1=scale_b[:], op=ALU.mult)
+
+        kgrp = {}
+        kbank = {}
+        kcodes = {}
+        kraw = (kcr, kpr)
+
+        def kt(c, kp, half):
+            bank = psum.tile([P, 2, 2, P], F32, name="tbank", bufs=3)
+            for i in range(2):
+                words = kraw[c][:, 2 * half + i, :].bitcast(F32)
+                for u in range(2):
+                    nc.tensor.transpose(bank[:, i, u, :], words[:, 256 * kp + u:256 * (kp + 1):2], ident[:])
+            kbank[c, kp, half] = bank
+
+        def ke(c, kp, half, e):
+            if (c, kp) not in kgrp:
+                kgrp[c, kp] = stage.tile([P, 4 * KEYS], BF16, name="kgrp%d%d" % (c, kp), bufs=1, align_bytes=64)
+            dst = kgrp[c, kp][:, 1024 * half:1024 * (half + 1)].bitcast(F32)
+            copy(e, dst.rearrange("p (i r u) -> p i r u", i=2, u=2), kbank[c, kp, half][:].rearrange("p i u r -> p i r u"))
+
+        def kq(c, kp):
+            codes = keep.tile([P, KEYS], U32, name="kcodes%d%d" % (c, kp), align_bytes=64)
+            scales = keep.tile([P, KEYS], U8, name="kscales%d%d" % (c, kp), align_bytes=64)
+            nc.vector.quantize_mx(out=codes[:].bitcast(FP8X4), scales=scales[:], in_=kgrp[c, kp][:])
+            kcodes[c, kp] = (codes, scales)
+
+        qbank = {}
+        qgrp = {}
+        qcodes = {}
+
+        def pj(c, g, h):
+            bank = psum.tile([P, 4, P], F32, name="qbank", bufs=3)
+            for t in range(4):
+                for kp in range(NPASS):
+                    wc, ws = wcodes[c, kp, g]
+                    xc, xs = xcodes[kp]
+                    nc.tensor.matmul_mx(
+                        out=bank[:, t, :],
+                        lhsT=wc[:, t * P:(t + 1) * P].bitcast(FP8X4), lhsT_scale=ws[:, t * P:(t + 1) * P],
+                        rhs=xc[:, h * P:(h + 1) * P].bitcast(FP8X4), rhs_scale=xs[:, h * P:(h + 1) * P],
+                        start=(kp == 0), stop=(kp == NPASS - 1))
+            qbank[c, g, h] = bank
+
+        def qe(c, g, h):
+            grp = stage.tile([P, P, 4], BF16, name="qgrp", bufs=6, align_bytes=64)
+            nc.vector.tensor_tensor(
+                out=grp[:], in0=qbank[c, g, h][:].rearrange("p t n -> p n t"),
+                in1=biases[c][:, g, :].unsqueeze(1).to_broadcast([P, P, 4]), op=ALU.add)
+            qgrp[c, g, h] = grp
+
+        def qq(c, g, h):
+            codes = keep.tile([P, P], U32, name="qcodes%d%d%d" % (c, g, h), align_bytes=64)
+            scales = keep.tile([P, P], U8, name="qscales%d%d%d" % (c, g, h), align_bytes=64)
+            nc.vector.quantize_mx(out=codes[:].bitcast(FP8X4), scales=scales[:], in_=qgrp[c, g, h][:].rearrange("p n t -> p (n t)"))
+            qcodes[c, g, h] = (codes, scales)
+
+        z = {}
+
+        def scr(c, g, h):
+            if g == 0:
+                z[c, h] = psum.tile([P, KEYS], F32, name="zbank%d" % h, bufs=1)
+            qc, qs = qcodes[c, g, h]
+            kc, ks = kcodes[c, g]
+            nc.tensor.matmul_mx(
+                out=z[c, h][:], lhsT=qc[:].bitcast(FP8X4), lhsT_scale=qs[:],
+                rhs=kc[:].bitcast(FP8X4), rhs_scale=ks[:], start=(g == 0), stop=(g == NGROUP - 1))
+
+        outs = (out_0, out_1)
+        nbs = {}
+        es = {}
+        sums = {}
+        recs = {}
+
+        def mx(c, h):
+            scaled = stage.tile([P, KEYS], BF16, name="scaled", bufs=2)
+            nb = stage.tile([P, 1], F32, name="nb", bufs=4)
+            nc.vector.tensor_scalar(out=scaled[:], in0=z[c, h][:], scalar1=-SCALE, scalar2=None,
+                                    op0=ALU.mult, op1=ALU.min, accum_out=nb[:])
+            nbs[c, h] = nb
+
+        def ex(c, h):
+            e = stage.tile([P, KEYS], F32, name="e", bufs=4)
+            s = stage.tile([P, 1], F32, name="s", bufs=4)
+            nc.scalar.activation(out=e[:], in_=z[c, h][:], func=ACT.Exp, bias=nbs[c, h][:], scale=SCALE, accum_out=s[:])
+            es[c, h] = e
+            sums[c, h] = s
+
+        def rc(c, h):
+            r = stage.tile([P, 1], F32, name="r", bufs=4)
+            nc.vector.reciprocal(out=r[:], in_=sums[c, h][:])
+            recs[c, h] = r
+
+        def nm(c, h):
+            o = stage.tile([P, KEYS], F32, name="o", bufs=4)
+            nc.vector.tensor_scalar(out=o[:], in0=es[c, h][:], scalar1=recs[c, h][:], scalar2=None, op0=ALU.mult)
+            nc.sync.dma_start(out=outs[c][h * P:(h + 1) * P, :], in_=o[:])
+
+        jobs = {"sc": sc, "pr": pr, "ilS": ilS, "ilV": ilV, "wq": wq, "xt": xt, "xe": xe, "xq": xq, "kt": kt, "ke": ke,
+                "kq": kq, "pj": pj, "qe": qe, "qq": qq, "scr": scr, "mx": mx, "ex": ex, "rc": rc, "nm": nm}
+        for job in ORDER:
+            jobs[job[0]](*job[1:])

@@ -255,21 +255,21 @@ def tile_executor_pa_kernel(tc, inst_embed, Wfc, bfc, Wfp, bfp, Kc, Kp_bytes, Kp
                 wgrp[w] = stage.tile([P, 4 * GROUP], BF16, name="wgrp", bufs=5, align_bytes=64)
             pr, kp, g = w
             raw = wraw[pr, kp][:, :, g * GROUP:(g + 1) * GROUP]
-            d = wgrp[w][:].rearrange("p (t m j) -> p t m j", t=4, j=4)
-            s = raw.rearrange("p j (m t) -> p t m j", t=4)
+            d = wgrp[w][:].rearrange("p (t m j) -> p m j t", t=4, j=4)
+            s = raw.rearrange("p j (m t) -> p m j t", t=4)
             return d, s
 
         def ilS(w):
             d, s = il_views(w)
-            cut = 4 - VQ[w]
+            cut = 32 * (4 - VQ[w])
             if cut:
                 nc.scalar.copy(out=d[:, 0:cut], in_=s[:, 0:cut])
 
         def ilV(w):
             d, s = il_views(w)
-            cut = 4 - VQ[w]
-            if cut < 4:
-                nc.vector.tensor_copy(out=d[:, cut:4], in_=s[:, cut:4])
+            cut = 32 * (4 - VQ[w])
+            if cut < 128:
+                nc.vector.tensor_copy(out=d[:, cut:128], in_=s[:, cut:128])
 
         def wq(w):
             codes = stage.tile([P, GROUP], U32, name="wcodes", bufs=13, align_bytes=64)

@@ -13,409 +13,342 @@ ALU = mybir.AluOpType
 ACT = mybir.ActivationFunctionType
 
 P = 128
-TOK = 256
+TOKENS = 256
 DIM = 1536
 KEYS = 512
 PASS = 512
-NPASS = DIM // PASS
 GROUP = 512
+NPASS = DIM // PASS
 NGROUP = DIM // GROUP
 SCALE = 1.0 / DIM ** 0.5
-FLOPS = 2 * TOK * DIM * DIM * 2 + 2 * TOK * KEYS * DIM * 2
+FLOPS = 2 * (2 * TOKENS * DIM * DIM) + 2 * (2 * TOKENS * KEYS * DIM)
 
-VQ = {(0, 1, 0): 1, (0, 1, 1): 0, (0, 2, 0): 4, (0, 2, 1): 2, (0, 1, 2): 4, (0, 2, 2): 0, (1, 0, 0): 0, (1, 1, 0): 0, (1, 2, 0): 0, (1, 0, 1): 4, (1, 1, 1): 4, (1, 2, 1): 2, (1, 0, 2): 1, (1, 1, 2): 0, (1, 2, 2): 0, (0, 0, 0): 4, (0, 0, 1): 0, (0, 0, 2): 0}
-LOADS = ("kp1", "002", "001", "kp0", "01*", "kc1", "x", "02*", "000", "kc0", "10*", "11*", "12*")
-ORDER = (
-    ("ilV", (0, 0, 2)),
-    ("sc", 0, "V"),
-    ("sc", 1, "S"),
-    ("ilV", (0, 0, 1)),
-    ("sc", 2, "V"),
-    ("ilS", (0, 0, 2)),
-    ("kt", 0, 0, 1),
-    ("pr", 2),
-    ("pr", 1),
-    ("pr", 3),
-    ("pr", 0),
-    ("ilS", (0, 0, 1)),
-    ("ilV", (0, 1, 2)),
-    ("ilS", (0, 1, 0)),
-    ("xt", 2),
-    ("xt", 1),
-    ("wq", (0, 0, 2)),
-    ("ilS", (0, 1, 1)),
-    ("ke", 0, 0, 1, "S"),
-    ("ilS", (0, 1, 2)),
-    ("xe", 2, "S"),
-    ("ilV", (0, 1, 0)),
-    ("wq", (0, 1, 2)),
-    ("xe", 1, "S"),
-    ("wq", (0, 0, 1)),
-    ("kt", 1, 1, 1),
-    ("xt", 0),
-    ("ke", 1, 1, 1, "S"),
-    ("ilS", (0, 2, 2)),
-    ("wq", (0, 1, 0)),
-    ("xe", 0, "S"),
-    ("kt", 1, 2, 0),
-    ("kt", 0, 1, 1),
-    ("ilV", (0, 1, 1)),
-    ("ke", 1, 2, 0, "S"),
-    ("ke", 0, 1, 1, "S"),
-    ("kt", 0, 0, 0),
-    ("wq", (0, 1, 1)),
-    ("kt", 0, 1, 0),
-    ("ilV", (0, 2, 2)),
-    ("ilS", (0, 2, 0)),
-    ("xq", 1),
-    ("ilV", (0, 2, 1)),
-    ("ilS", (0, 0, 0)),
-    ("ilV", (0, 2, 0)),
-    ("kt", 0, 2, 1),
-    ("ilV", (0, 0, 0)),
-    ("ke", 0, 0, 0, "S"),
-    ("ilS", (1, 0, 1)),
-    ("ilS", (0, 2, 1)),
-    ("wq", (0, 2, 0)),
-    ("xq", 0),
-    ("xq", 2),
-    ("wq", (0, 0, 0)),
-    ("kq", 0, 0),
-    ("kt", 0, 2, 0),
-    ("pj", 0, 0, 0),
-    ("wq", (0, 2, 2)),
-    ("wq", (0, 2, 1)),
-    ("ke", 0, 1, 0, "S"),
-    ("ilV", (1, 0, 1)),
-    ("pj", 0, 0, 1),
-    ("pj", 0, 1, 0),
-    ("ke", 0, 2, 1, "S"),
-    ("qe", 0, 0, 0),
-    ("kt", 1, 0, 1),
-    ("kt", 1, 0, 0),
-    ("ilV", (1, 0, 2)),
-    ("ilV", (1, 1, 0)),
-    ("qq", 0, 0, 0),
-    ("ke", 0, 2, 0, "S"),
-    ("kq", 0, 1),
-    ("ilS", (1, 0, 0)),
-    ("wq", (1, 0, 1)),
-    ("pj", 0, 1, 1),
-    ("qe", 0, 0, 1),
-    ("ilS", (1, 0, 2)),
-    ("ilV", (1, 1, 1)),
-    ("wq", (1, 0, 2)),
-    ("qq", 0, 0, 1),
-    ("scr", 0, 0, 0),
-    ("pj", 0, 2, 0),
-    ("ilS", (1, 1, 1)),
-    ("wq", (1, 1, 1)),
-    ("scr", 0, 0, 1),
-    ("kq", 0, 2),
-    ("kt", 1, 2, 1),
-    ("qe", 0, 1, 0),
-    ("ilV", (1, 2, 1)),
-    ("ke", 1, 0, 0, "S"),
-    ("ilV", (1, 0, 0)),
-    ("ilS", (1, 1, 0)),
-    ("pj", 0, 2, 1),
-    ("ilS", (1, 2, 1)),
-    ("qq", 0, 1, 0),
-    ("ilV", (1, 2, 0)),
-    ("qe", 0, 2, 0),
-    ("wq", (1, 0, 0)),
-    ("qe", 0, 1, 1),
-    ("wq", (1, 2, 1)),
-    ("scr", 0, 1, 0),
-    ("wq", (1, 1, 0)),
-    ("ke", 1, 0, 1, "S"),
-    ("qq", 0, 2, 0),
-    ("pj", 1, 1, 0),
-    ("pj", 1, 1, 1),
-    ("scr", 0, 2, 0),
-    ("ilS", (1, 2, 0)),
-    ("ilV", (1, 1, 2)),
-    ("ilS", (1, 2, 2)),
-    ("qq", 0, 1, 1),
-    ("ilV", (1, 2, 2)),
-    ("kq", 1, 0),
-    ("wq", (1, 2, 0)),
-    ("qe", 0, 2, 1),
-    ("pj", 1, 0, 1),
-    ("qe", 1, 1, 0),
-    ("pj", 1, 0, 0),
-    ("mx", 0, 0),
-    ("qe", 1, 1, 1),
-    ("qe", 1, 0, 1),
-    ("ilS", (1, 1, 2)),
-    ("qq", 1, 1, 0),
-    ("wq", (1, 2, 2)),
-    ("qq", 0, 2, 1),
-    ("qq", 1, 0, 1),
-    ("scr", 0, 1, 1),
-    ("qe", 1, 0, 0),
-    ("wq", (1, 1, 2)),
-    ("kt", 1, 1, 0),
-    ("scr", 0, 2, 1),
-    ("ke", 1, 2, 1, "S"),
-    ("mx", 0, 1),
-    ("pj", 1, 2, 0),
-    ("ex", 0, 0),
-    ("rc", 0, 0),
-    ("qq", 1, 0, 0),
-    ("kq", 1, 2),
-    ("pj", 1, 2, 1),
-    ("scr", 1, 0, 0),
-    ("qe", 1, 2, 0),
-    ("ke", 1, 1, 0, "S"),
-    ("kq", 1, 1),
-    ("qq", 1, 2, 0),
-    ("scr", 1, 1, 0),
-    ("ex", 0, 1),
-    ("scr", 1, 0, 1),
-    ("scr", 1, 2, 0),
-    ("qq", 1, 1, 1),
-    ("qe", 1, 2, 1),
-    ("nm", 0, 0),
-    ("scr", 1, 1, 1),
-    ("qq", 1, 2, 1),
-    ("scr", 1, 2, 1),
-    ("mx", 1, 0),
-    ("ex", 1, 0),
-    ("mx", 1, 1),
-    ("rc", 0, 1),
-    ("rc", 1, 0),
-    ("nm", 1, 0),
-    ("ex", 1, 1),
-    ("rc", 1, 1),
-    ("nm", 0, 1),
-    ("nm", 1, 1),
+LOADS = (
+    ("weights", 0, 0, (0,)),
+    ("weights", 0, 2, (1,)),
+    ("embedding",),
+    ("keys", 1, 0),
+    ("weights", 0, 2, (2,)),
+    ("keys", 1, 1),
+    ("weights", 0, 2, (0,)),
+    ("weights", 0, 1, (0, 1, 2)),
+    ("keys", 0, 0),
+    ("biases",),
+    ("weights", 0, 0, (1, 2)),
+    ("weights", 1, 0, (0,)),
+    ("keys", 0, 1),
+    ("weights", 1, 1, (0, 1, 2)),
+    ("weights", 1, 2, (0, 1, 2)),
+    ("weights", 1, 0, (1, 2)),
+)
+
+WEIGHT_BUFFERS = {1: 4, 2: 1, 3: 3}
+
+PIECES = (
+    ((0, 0, 0), "SVVV"),
+    ((0, 2, 1), "VVVV"),
+    ((0, 2, 2), "SSSS"),
+    ((0, 2, 0), "SSSS"),
+    ((0, 1, 1), "SSSS"),
+    ((0, 1, 0), "VVVV"),
+    ((0, 1, 2), "VVVV"),
+    ((0, 0, 1), "SSSS"),
+    ((1, 0, 0), "SSVV"),
+    ((0, 0, 2), "VVVV"),
+    ((1, 1, 0), "SSSS"),
+    ((1, 2, 0), "VVVV"),
+    ((1, 1, 1), "SSSS"),
+    ((1, 2, 1), "SSSS"),
+    ((1, 0, 1), "SSSS"),
+    ((1, 1, 2), "VVVV"),
+    ((1, 0, 2), "SSSS"),
+    ((1, 2, 2), "SSSS"),
+)
+LAST_PIECE = (1, 2, 2)
+
+STEPS = (
+    (("spread_scale", 0), ("spread_scale", 1), ("spread_scale", 2),),
+    (("quantize_weights", 0, 0, 0), ("quantize_weights", 0, 2, 1), ("scale_keys", 0), ("turn_embedding", 0),
+     ("turn_embedding", 1), ("turn_embedding", 2), ("quantize_embedding", 1),),
+    (("scale_keys", 1), ("scale_keys", 2),),
+    (("scale_keys", 3), ("turn_keys", 1, 0, 0), ("turn_keys", 1, 1, 0), ("turn_keys", 1, 1, 1),),
+    (("turn_keys", 1, 0, 1), ("quantize_embedding", 0), ("quantize_embedding", 2),),
+    (),
+    (("quantize_weights", 0, 1, 0), ("quantize_weights", 0, 2, 0), ("quantize_weights", 0, 2, 2),
+     ("turn_keys", 0, 2, 0),),
+    (("quantize_weights", 0, 1, 1), ("quantize_weights", 0, 1, 2), ("turn_keys", 0, 0, 0),
+     ("turn_keys", 0, 1, 0), ("quantize_keys", 1, 0), ("project", 0, 0, 0), ("project", 0, 0, 1),),
+    (("add_bias", 0, 0, 0), ("turn_keys", 0, 0, 1), ("turn_keys", 0, 2, 1), ("quantize_keys", 1, 1),),
+    (("quantize_weights", 0, 0, 1), ("quantize_weights", 0, 0, 2), ("quantize_weights", 1, 0, 0),
+     ("add_bias", 0, 0, 1), ("turn_keys", 0, 1, 1), ("quantize_keys", 0, 2), ("quantize_query", 0, 0, 0),
+     ("quantize_query", 0, 0, 1), ("project", 0, 1, 0), ("project", 0, 2, 0), ("project", 0, 2, 1),),
+    (("add_bias", 0, 1, 0), ("add_bias", 0, 2, 0), ("quantize_keys", 0, 0),),
+    (("quantize_weights", 1, 1, 0), ("quantize_weights", 1, 2, 0), ("score", 0, 0, 1),),
+    (("add_bias", 0, 2, 1), ("quantize_keys", 0, 1), ("project", 0, 1, 1), ("project", 1, 0, 1),
+     ("score", 0, 0, 0),),
+    (("quantize_weights", 1, 1, 1), ("add_bias", 0, 1, 1), ("quantize_query", 0, 2, 0),
+     ("quantize_query", 0, 2, 1),),
+    (("quantize_query", 0, 1, 0), ("quantize_query", 0, 1, 1), ("project", 1, 0, 0),),
+    (("add_bias", 1, 0, 0), ("score", 0, 1, 0),),
+    (("quantize_weights", 1, 0, 1), ("quantize_weights", 1, 1, 2), ("quantize_weights", 1, 2, 1),
+     ("add_bias", 1, 0, 1), ("score", 0, 1, 1), ("score", 0, 2, 0), ("score", 0, 2, 1), ("row_max", 0, 0),
+     ("row_max", 0, 1),),
+    (("turn_keys", 1, 2, 1), ("quantize_query", 1, 0, 0), ("quantize_query", 1, 0, 1), ("exponent", 0, 1),),
+    (("quantize_weights", 1, 0, 2), ("turn_keys", 1, 2, 0), ("project", 1, 1, 0), ("project", 1, 1, 1),
+     ("exponent", 0, 0),),
+    (("quantize_last_weights", 0), ("quantize_last_weights", 1), ("add_bias", 1, 1, 0), ("add_bias", 1, 1, 1),
+     ("quantize_query", 1, 1, 0), ("project_last", 0, 0), ("project_last", 0, 1),),
+    (("add_bias", 1, 2, 0), ("quantize_keys", 1, 2), ("quantize_query", 1, 2, 0), ("project_last", 1, 0),
+     ("project_last", 1, 1), ("score", 1, 0, 0), ("score", 1, 0, 1), ("score", 1, 1, 0), ("score", 1, 2, 0),
+     ("normalise", 0, 0),),
+    (("add_bias", 1, 2, 1), ("quantize_query", 1, 1, 1), ("quantize_query", 1, 2, 1), ("score", 1, 1, 1),
+     ("score", 1, 2, 1), ("row_max", 1, 0), ("row_max", 1, 1), ("exponent", 1, 0), ("exponent", 1, 1),
+     ("normalise", 0, 1), ("normalise", 1, 0), ("normalise", 1, 1),),
 )
 
 
 def tile_executor_pa_kernel(tc, inst_embed, Wfc, bfc, Wfp, bfp, Kc, Kp_bytes, Kp_scale, out_0, out_1):
     nc = tc.nc
+    weights = (Wfc, Wfp)
+    outs = (out_0, out_1)
+
     with ExitStack() as ctx:
-        keep = ctx.enter_context(tc.tile_pool(name="keep", bufs=1))
-        wpool = ctx.enter_context(tc.tile_pool(name="wpool", bufs=5))
-        stage = ctx.enter_context(tc.tile_pool(name="stage", bufs=3))
+        sbuf = ctx.enter_context(tc.tile_pool(name="sbuf", bufs=1))
         psum = ctx.enter_context(tc.psum_pool(name="psum", bufs=1))
         ctx.enter_context(tc.manual_schedule())
 
-        scale_col = keep.tile([P, NPASS, 4], F32, name="scale_col", align_bytes=64)
+        used = {}
+
+        def turn_name(name, count):
+            turn = used.get(name, 0)
+            used[name] = turn + 1
+            return "%s_%d" % (name, turn % count)
+
+        def rotate(shape, dtype, name, count):
+            return sbuf.tile(shape, dtype, name=turn_name(name, count), align_bytes=64)
+
+        def bank_of(shape, dtype, name, count):
+            return psum.tile(shape, dtype, name=turn_name(name, count))
+
+        def keep(shape, dtype, name):
+            return sbuf.tile(shape, dtype, name=name, align_bytes=64)
+
+        scale_col = keep([P, NPASS, 4], F32, "scale_col")
         nc.scalar.dma_start(out=scale_col[:], in_=Kp_scale.rearrange("o (g p t) -> p (o g) t", p=P, t=4))
-        ident = keep.tile([P, P], F32, name="ident", align_bytes=64)
+
+        ident = keep([P, P], F32, "ident")
         make_identity(nc, ident[:])
-        warm = keep.tile([P, 1], F32, name="warm")
-        nc.vector.memset(warm[:], 0.0)
-        warm2 = keep.tile([P, 1], F32, name="warm2")
-        nc.scalar.activation(out=warm2[:], in_=warm[:], func=ACT.Exp)
 
-        W = (Wfc, Wfp)
-        wraw = {}
-        xraw = keep.tile([P, 2, DIM], BF16, name="xraw", align_bytes=64)
-        kpb = keep.tile([P, 4, DIM], U8, name="kpb", align_bytes=64)
-        kcr = keep.tile([P, 4, DIM], BF16, name="kcr", align_bytes=64)
-        biases = []
-        count = 0
-        for d in LOADS:
-            if d[0] == "k":
-                half = int(d[2])
-                if d[1] == "p":
-                    nc.sync.dma_start(out=kpb[:, 2 * half:2 * half + 2, :], in_=Kp_bytes.rearrange("(b p) k -> p b k", p=P)[:, 2 * half:2 * half + 2, :])
-                else:
-                    nc.sync.dma_start(out=kcr[:, 2 * half:2 * half + 2, :], in_=Kc.rearrange("(b p) k -> p b k", p=P)[:, 2 * half:2 * half + 2, :])
-            elif d == "x":
-                nc.sync.dma_start(out=xraw[:], in_=inst_embed.rearrange("(h p) k -> p h k", p=P))
-            else:
-                pr = int(d[0])
-                kp = int(d[1])
-                if (pr, kp) not in wraw:
-                    t = wpool.tile([P, 4, DIM], BF16, name="wraw", align_bytes=64)
-                    wraw[pr, kp] = t
-                t = wraw[pr, kp]
-                src = W[pr][kp * PASS:(kp + 1) * PASS, :].rearrange("(p j) n -> p j n", j=4)
-                if d[2] == "*":
-                    nc.sync.dma_start(out=t[:], in_=src)
-                else:
-                    g = int(d[2])
-                    nc.sync.dma_start(out=t[:, :, 512 * g:512 * g + 512], in_=src[:, :, 512 * g:512 * g + 512])
-            count += 1
-            if count == 6:
-                for i, b in enumerate((bfc, bfp)):
-                    bt = keep.tile([P, NGROUP, 4], BF16, name="bias%d" % i, align_bytes=64)
-                    nc.sync.dma_start(out=bt[:], in_=b.rearrange("(g p t) -> p g t", p=P, t=4))
-                    biases.append(bt)
+        warm_in = keep([P, 1], F32, "warm_in")
+        nc.vector.memset(warm_in[:], 0.0)
+        warm_out = keep([P, 1], F32, "warm_out")
+        nc.scalar.activation(out=warm_out[:], in_=warm_in[:], func=ACT.Exp)
 
-        wgrp = {}
-        wcodes = {}
+        raw_weights = {}
+        raw_keys = {}
+        bias = {}
+        embedding = keep([P, 2, DIM], BF16, "embedding")
 
-        def il_views(w):
-            if w not in wgrp:
-                wgrp[w] = stage.tile([P, 4 * GROUP], BF16, name="wgrp", bufs=5, align_bytes=64)
-            pr, kp, g = w
-            raw = wraw[pr, kp][:, :, g * GROUP:(g + 1) * GROUP]
-            d = wgrp[w][:].rearrange("p (t m j) -> p m j t", t=4, j=4)
-            s = raw.rearrange("p j (m t) -> p m j t", t=4)
-            return d, s
+        def load_weights(c, kp, groups):
+            rows = weights[c][kp * PASS:(kp + 1) * PASS, :].rearrange("(p j) n -> p j n", j=4)
+            n = len(groups)
+            tile = rotate([P, 4, n * GROUP], BF16, "weights_%d" % n, WEIGHT_BUFFERS[n])
+            nc.sync.dma_start(out=tile[:], in_=rows[:, :, groups[0] * GROUP:(groups[-1] + 1) * GROUP])
+            for i, g in enumerate(groups):
+                raw_weights[c, kp, g] = tile[:, :, i * GROUP:(i + 1) * GROUP]
 
-        def ilS(w):
-            d, s = il_views(w)
-            cut = 32 * (4 - VQ[w])
-            if cut:
-                nc.scalar.copy(out=d[:, 0:cut], in_=s[:, 0:cut])
+        def load_keys(c, half):
+            rows = (Kc, Kp_bytes)[c].rearrange("(b p) k -> p b k", p=P)[:, 2 * half:2 * half + 2, :]
+            tile = keep([P, 2, DIM], (BF16, U8)[c], ("keys_%d", "key_bytes_%d")[c] % half)
+            nc.sync.dma_start(out=tile[:], in_=rows)
+            raw_keys[c, half] = tile
 
-        def ilV(w):
-            d, s = il_views(w)
-            cut = 32 * (4 - VQ[w])
-            if cut < 128:
-                nc.vector.tensor_copy(out=d[:, cut:128], in_=s[:, cut:128])
+        def load_embedding():
+            nc.sync.dma_start(out=embedding[:], in_=inst_embed.rearrange("(h p) k -> p h k", p=P))
 
-        def wq(w):
-            codes = stage.tile([P, GROUP], U32, name="wcodes", bufs=13, align_bytes=64)
-            scales = stage.tile([P, GROUP], U8, name="wscales", bufs=13, align_bytes=64)
-            nc.vector.quantize_mx(out=codes[:].bitcast(FP8X4), scales=scales[:], in_=wgrp[w][:])
-            wcodes[w] = (codes, scales)
+        def load_biases():
+            for c, vector in enumerate((bfc, bfp)):
+                bias[c] = keep([P, NGROUP, 4], BF16, "bias_%d" % c)
+                nc.sync.dma_start(out=bias[c][:], in_=vector.rearrange("(g p t) -> p g t", p=P, t=4))
 
-        def copy(e, out, in_):
-            if e == "S":
-                nc.scalar.copy(out=out, in_=in_)
-            else:
+        loads = {"weights": load_weights, "keys": load_keys, "embedding": load_embedding, "biases": load_biases}
+        for load in LOADS:
+            loads[load[0]](*load[1:])
+
+        def copy(out, in_, on_vector):
+            if on_vector:
                 nc.vector.tensor_copy(out=out, in_=in_)
+            else:
+                nc.scalar.copy(out=out, in_=in_)
 
-        xcodes = {}
-        xbank = {}
-        xgrp = keep.tile([P, NPASS, 4 * TOK], BF16, name="xgrp", align_bytes=64)
+        def quantize(grouped, name, count=0):
+            width = grouped.shape[1] // 4
+            if count:
+                codes = rotate([P, width], U32, name + "_codes", count)
+                scales = rotate([P, width], U8, name + "_scales", count)
+            else:
+                codes = keep([P, width], U32, name + "_codes")
+                scales = keep([P, width], U8, name + "_scales")
+            nc.vector.quantize_mx(out=codes[:].bitcast(FP8X4), scales=scales[:], in_=grouped)
+            return codes, scales
 
-        def xt(g):
-            bank = psum.tile([P, 2, 2, P], F32, name="tbank", bufs=3)
+        def turning_bank():
+            return bank_of([P, 4, P], F32, "turning", 3)
+
+        grouped_weights = {}
+        weight_codes = {}
+
+        def interleave(piece, shares):
+            grouped = rotate([P, 4 * GROUP], BF16, "grouped", 5)
+            grouped_weights[piece] = grouped
+            rows = raw_weights[piece].rearrange("p j (m t) -> p m j t", t=4)
+            by_m = grouped[:].rearrange("p (t m j) -> p m j t", t=4, j=4)
+            for letter in ("S", "V"):
+                if letter in shares:
+                    m0 = 32 * shares.index(letter)
+                    m1 = m0 + 32 * len([s for s in shares if s == letter])
+                    copy(by_m[:, m0:m1], rows[:, m0:m1], letter == "V")
+
+        def quantize_weights(c, kp, g):
+            codes, scales = quantize(grouped_weights[c, kp, g][:], "weight", 13)
+            for t in range(4):
+                cols = slice(t * P, (t + 1) * P)
+                weight_codes[(c, kp, g), t] = (codes[:, cols], scales[:, cols])
+
+        def quantize_last_weights(half):
+            codes, scales = quantize(grouped_weights[LAST_PIECE][:, 1024 * half:1024 * (half + 1)], "last_weight_%d" % half)
+            for i in range(2):
+                cols = slice(i * P, (i + 1) * P)
+                weight_codes[LAST_PIECE, 2 * half + i] = (codes[:, cols], scales[:, cols])
+
+        grouped_embedding = {}
+        embedding_codes = {}
+
+        def turn_embedding(g, on_vector=False):
+            bank = turning_bank()
             for h in range(2):
-                words = xraw[:, h, :].bitcast(F32)
+                words = embedding[:, h, :].bitcast(F32)
                 for u in range(2):
-                    nc.tensor.transpose(bank[:, h, u, :], words[:, 256 * g + u:256 * (g + 1):2], ident[:])
-            xbank[g] = bank
+                    nc.tensor.transpose(bank[:, 2 * h + u, :], words[:, 256 * g + u:256 * (g + 1):2], ident[:])
+            grouped_embedding[g] = keep([P, 4 * TOKENS], BF16, "grouped_embedding_%d" % g)
+            copy(grouped_embedding[g][:].bitcast(F32).rearrange("p (h r u) -> p h r u", h=2, u=2),
+                 bank[:].rearrange("p (h u) r -> p h r u", u=2), on_vector)
 
-        def xe(g, e):
-            copy(e, xgrp[:, g, :].bitcast(F32).rearrange("p (h r u) -> p h r u", h=2, u=2),
-                 xbank[g][:].rearrange("p h u r -> p h r u"))
+        def quantize_embedding(g):
+            embedding_codes[g] = quantize(grouped_embedding[g][:], "embedding_%d" % g)
 
-        def xq(g):
-            codes = keep.tile([P, TOK], U32, name="xcodes%d" % g, align_bytes=64)
-            scales = keep.tile([P, TOK], U8, name="xscales%d" % g, align_bytes=64)
-            nc.vector.quantize_mx(out=codes[:].bitcast(FP8X4), scales=scales[:], in_=xgrp[:, g, :])
-            xcodes[g] = (codes, scales)
+        scale_row = keep([P, DIM], F32, "scale_row")
+        scaled_keys = {}
+        grouped_keys = {}
+        key_codes = {}
 
-        scale_b = keep.tile([P, DIM], F32, name="scale_b", align_bytes=64)
-
-        def sc(g, e):
-            bank = psum.tile([P, 4, P], F32, name="tbank", bufs=3)
+        def spread_scale(g, on_vector=False):
+            bank = turning_bank()
             for t in range(4):
                 nc.tensor.transpose(bank[:, t, :], scale_col[:, g, t:t + 1].to_broadcast([P, P]), ident[:])
-            copy(e, scale_b[:, g * PASS:(g + 1) * PASS].rearrange("p (n t) -> p n t", t=4),
-                 bank[:].rearrange("p t n -> p n t"))
+            copy(scale_row[:, g * PASS:(g + 1) * PASS].rearrange("p (n t) -> p n t", t=4),
+                 bank[:].rearrange("p t n -> p n t"), on_vector)
 
-        kpr = keep.tile([P, 4, DIM], BF16, name="kpr", align_bytes=64)
+        def scale_keys(b):
+            scaled_keys[b] = keep([P, DIM], BF16, "scaled_keys_%d" % b)
+            nc.vector.tensor_tensor(out=scaled_keys[b][:], in0=raw_keys[1, b // 2][:, b % 2, :].bitcast(FP8),
+                                    in1=scale_row[:], op=ALU.mult)
 
-        def pr(b):
-            nc.vector.tensor_tensor(out=kpr[:, b, :], in0=kpb[:, b, :].bitcast(FP8), in1=scale_b[:], op=ALU.mult)
-
-        kgrp = {}
-        kbank = {}
-        kcodes = {}
-        kraw = (kcr, kpr)
-
-        def kt(c, kp, half):
-            bank = psum.tile([P, 2, 2, P], F32, name="tbank", bufs=3)
+        def turn_keys(c, g, half, on_vector=False):
+            bank = turning_bank()
             for i in range(2):
-                words = kraw[c][:, 2 * half + i, :].bitcast(F32)
+                words = (scaled_keys[2 * half + i][:] if c else raw_keys[0, half][:, i, :]).bitcast(F32)
                 for u in range(2):
-                    nc.tensor.transpose(bank[:, i, u, :], words[:, 256 * kp + u:256 * (kp + 1):2], ident[:])
-            kbank[c, kp, half] = bank
+                    nc.tensor.transpose(bank[:, 2 * i + u, :], words[:, 256 * g + u:256 * (g + 1):2], ident[:])
+            if (c, g) not in grouped_keys:
+                grouped_keys[c, g] = keep([P, 4 * KEYS], BF16, "grouped_keys_%d%d" % (c, g))
+            words = grouped_keys[c, g][:, 1024 * half:1024 * (half + 1)].bitcast(F32)
+            copy(words.rearrange("p (i r u) -> p i r u", i=2, u=2), bank[:].rearrange("p (i u) r -> p i r u", u=2), on_vector)
 
-        def ke(c, kp, half, e):
-            if (c, kp) not in kgrp:
-                kgrp[c, kp] = stage.tile([P, 4 * KEYS], BF16, name="kgrp%d%d" % (c, kp), bufs=1, align_bytes=64)
-            dst = kgrp[c, kp][:, 1024 * half:1024 * (half + 1)].bitcast(F32)
-            copy(e, dst.rearrange("p (i r u) -> p i r u", i=2, u=2), kbank[c, kp, half][:].rearrange("p i u r -> p i r u"))
+        def quantize_keys(c, g):
+            key_codes[c, g] = quantize(grouped_keys[c, g][:], "key_%d%d" % (c, g))
 
-        def kq(c, kp):
-            codes = keep.tile([P, KEYS], U32, name="kcodes%d%d" % (c, kp), align_bytes=64)
-            scales = keep.tile([P, KEYS], U8, name="kscales%d%d" % (c, kp), align_bytes=64)
-            nc.vector.quantize_mx(out=codes[:].bitcast(FP8X4), scales=scales[:], in_=kgrp[c, kp][:])
-            kcodes[c, kp] = (codes, scales)
+        query_bank = {}
+        grouped_query = {}
+        query_codes = {}
 
-        qbank = {}
-        qgrp = {}
-        qcodes = {}
-
-        def pj(c, g, h):
-            bank = psum.tile([P, 4, P], F32, name="qbank", bufs=3)
-            for t in range(4):
+        def project_slots(c, g, h, slots):
+            for t in slots:
                 for kp in range(NPASS):
-                    wc, ws = wcodes[c, kp, g]
-                    xc, xs = xcodes[kp]
+                    w_codes, w_scales = weight_codes[(c, kp, g), t]
+                    x_codes, x_scales = embedding_codes[kp]
                     nc.tensor.matmul_mx(
-                        out=bank[:, t, :],
-                        lhsT=wc[:, t * P:(t + 1) * P].bitcast(FP8X4), lhsT_scale=ws[:, t * P:(t + 1) * P],
-                        rhs=xc[:, h * P:(h + 1) * P].bitcast(FP8X4), rhs_scale=xs[:, h * P:(h + 1) * P],
+                        out=query_bank[c, g, h][:, t, :],
+                        lhsT=w_codes.bitcast(FP8X4), lhsT_scale=w_scales,
+                        rhs=x_codes[:, h * P:(h + 1) * P].bitcast(FP8X4), rhs_scale=x_scales[:, h * P:(h + 1) * P],
                         start=(kp == 0), stop=(kp == NPASS - 1))
-            qbank[c, g, h] = bank
 
-        def qe(c, g, h):
-            grp = stage.tile([P, P, 4], BF16, name="qgrp", bufs=6, align_bytes=64)
+        def project(c, g, h):
+            query_bank[c, g, h] = bank_of([P, 4, P], F32, "query", 3)
+            project_slots(c, g, h, (0, 1, 2, 3))
+
+        def project_last(h, half):
+            c, _, g = LAST_PIECE
+            if half == 0:
+                query_bank[c, g, h] = bank_of([P, 4, P], F32, "query", 3)
+            project_slots(c, g, h, (2 * half, 2 * half + 1))
+
+        def add_bias(c, g, h):
+            grouped = rotate([P, P, 4], BF16, "grouped_query", 6)
             nc.vector.tensor_tensor(
-                out=grp[:], in0=qbank[c, g, h][:].rearrange("p t n -> p n t"),
-                in1=biases[c][:, g, :].unsqueeze(1).to_broadcast([P, P, 4]), op=ALU.add)
-            qgrp[c, g, h] = grp
+                out=grouped[:], in0=query_bank[c, g, h][:].rearrange("p t n -> p n t"),
+                in1=bias[c][:, g, :].unsqueeze(1).to_broadcast([P, P, 4]), op=ALU.add)
+            grouped_query[c, g, h] = grouped
 
-        def qq(c, g, h):
-            codes = keep.tile([P, P], U32, name="qcodes%d%d%d" % (c, g, h), align_bytes=64)
-            scales = keep.tile([P, P], U8, name="qscales%d%d%d" % (c, g, h), align_bytes=64)
-            nc.vector.quantize_mx(out=codes[:].bitcast(FP8X4), scales=scales[:], in_=qgrp[c, g, h][:].rearrange("p n t -> p (n t)"))
-            qcodes[c, g, h] = (codes, scales)
+        def quantize_query(c, g, h):
+            query_codes[c, g, h] = quantize(grouped_query[c, g, h][:].rearrange("p n t -> p (n t)"), "query_%d%d%d" % (c, g, h))
 
-        z = {}
-
-        def scr(c, g, h):
-            if g == 0:
-                z[c, h] = psum.tile([P, KEYS], F32, name="zbank%d" % h, bufs=1)
-            qc, qs = qcodes[c, g, h]
-            kc, ks = kcodes[c, g]
-            nc.tensor.matmul_mx(
-                out=z[c, h][:], lhsT=qc[:].bitcast(FP8X4), lhsT_scale=qs[:],
-                rhs=kc[:].bitcast(FP8X4), rhs_scale=ks[:], start=(g == 0), stop=(g == NGROUP - 1))
-
-        outs = (out_0, out_1)
-        nbs = {}
-        es = {}
+        score_bank = {}
+        summed = {}
+        neg_max = {}
+        exponents = {}
         sums = {}
-        recs = {}
 
-        def mx(c, h):
-            scaled = stage.tile([P, KEYS], BF16, name="scaled", bufs=2)
-            nb = stage.tile([P, 1], F32, name="nb", bufs=4)
-            nc.vector.tensor_scalar(out=scaled[:], in0=z[c, h][:], scalar1=-SCALE, scalar2=None,
-                                    op0=ALU.mult, op1=ALU.min, accum_out=nb[:])
-            nbs[c, h] = nb
+        def score(c, g, h):
+            if (c, h) not in summed:
+                score_bank[c, h] = psum.tile([P, KEYS], F32, name="score_%d" % h)
+                summed[c, h] = 0
+            q_codes, q_scales = query_codes[c, g, h]
+            k_codes, k_scales = key_codes[c, g]
+            nc.tensor.matmul_mx(
+                out=score_bank[c, h][:], lhsT=q_codes[:].bitcast(FP8X4), lhsT_scale=q_scales[:],
+                rhs=k_codes[:].bitcast(FP8X4), rhs_scale=k_scales[:],
+                start=(summed[c, h] == 0), stop=(summed[c, h] == NGROUP - 1))
+            summed[c, h] += 1
 
-        def ex(c, h):
-            e = stage.tile([P, KEYS], F32, name="e", bufs=4)
-            s = stage.tile([P, 1], F32, name="s", bufs=4)
-            nc.scalar.activation(out=e[:], in_=z[c, h][:], func=ACT.Exp, bias=nbs[c, h][:], scale=SCALE, accum_out=s[:])
-            es[c, h] = e
-            sums[c, h] = s
+        def row_max(c, h):
+            unused = rotate([P, KEYS], BF16, "unused", 2)
+            neg_max[c, h] = keep([P, 1], F32, "neg_max_%d%d" % (c, h))
+            nc.vector.tensor_scalar(out=unused[:], in0=score_bank[c, h][:], scalar1=-SCALE, scalar2=None,
+                                    op0=ALU.mult, op1=ALU.min, accum_out=neg_max[c, h][:])
 
-        def rc(c, h):
-            r = stage.tile([P, 1], F32, name="r", bufs=4)
-            nc.vector.reciprocal(out=r[:], in_=sums[c, h][:])
-            recs[c, h] = r
+        def exponent(c, h):
+            exponents[c, h] = keep([P, KEYS], F32, "exponent_%d" % h)
+            sums[c, h] = keep([P, 1], F32, "sum_%d%d" % (c, h))
+            nc.scalar.activation(out=exponents[c, h][:], in_=score_bank[c, h][:], func=ACT.Exp,
+                                 bias=neg_max[c, h][:], scale=SCALE, accum_out=sums[c, h][:])
 
-        def nm(c, h):
-            o = stage.tile([P, KEYS], F32, name="o", bufs=4)
-            nc.vector.tensor_scalar(out=o[:], in0=es[c, h][:], scalar1=recs[c, h][:], scalar2=None, op0=ALU.mult)
-            nc.sync.dma_start(out=outs[c][h * P:(h + 1) * P, :], in_=o[:])
+        def normalise(c, h):
+            factor = keep([P, 1], F32, "factor_%d%d" % (c, h))
+            nc.vector.reciprocal(out=factor[:], in_=sums[c, h][:])
+            result = keep([P, KEYS], F32, "result_%d%d" % (c, h))
+            nc.vector.tensor_scalar(out=result[:], in0=exponents[c, h][:], scalar1=factor[:], scalar2=None, op0=ALU.mult)
+            nc.sync.dma_start(out=outs[c][h * P:(h + 1) * P, :], in_=result[:])
 
-        jobs = {"sc": sc, "pr": pr, "ilS": ilS, "ilV": ilV, "wq": wq, "xt": xt, "xe": xe, "xq": xq, "kt": kt, "ke": ke,
-                "kq": kq, "pj": pj, "qe": qe, "qq": qq, "scr": scr, "mx": mx, "ex": ex, "rc": rc, "nm": nm}
-        for job in ORDER:
-            jobs[job[0]](*job[1:])
+        jobs = {
+            "quantize_weights": quantize_weights, "quantize_last_weights": quantize_last_weights,
+            "turn_embedding": turn_embedding, "quantize_embedding": quantize_embedding,
+            "spread_scale": spread_scale, "scale_keys": scale_keys, "turn_keys": turn_keys, "quantize_keys": quantize_keys,
+            "project": project, "project_last": project_last, "add_bias": add_bias, "quantize_query": quantize_query,
+            "score": score, "row_max": row_max, "exponent": exponent, "normalise": normalise,
+        }
+        for i, step in enumerate(STEPS):
+            if i < len(PIECES):
+                interleave(*PIECES[i])
+            for job in step:
+                jobs[job[0]](*job[1:])

from contextlib import ExitStack

import concourse.mybir as mybir
from concourse.masks import make_identity

F32 = mybir.dt.float32
BF16 = mybir.dt.bfloat16
U32 = mybir.dt.uint32
U8 = mybir.dt.uint8
FP8 = mybir.dt.float8_e4m3fn
FP8X4 = mybir.dt.float8_e4m3fn_x4
ALU = mybir.AluOpType
ACT = mybir.ActivationFunctionType

P = 128
TOKENS = 256
DIM = 1536
KEYS = 512
PASS = 512
GROUP = 512
NPASS = DIM // PASS
NGROUP = DIM // GROUP
SCALE = 1.0 / DIM ** 0.5
FLOPS = 2 * (2 * TOKENS * DIM * DIM) + 2 * (2 * TOKENS * KEYS * DIM)

LOADS = (
    ("weights", 0, 0, (0,)),
    ("weights", 0, 2, (1,)),
    ("embedding",),
    ("keys", 1, 0),
    ("weights", 0, 2, (2,)),
    ("keys", 1, 1),
    ("weights", 0, 2, (0,)),
    ("weights", 0, 1, (0, 1, 2)),
    ("keys", 0, 0),
    ("biases",),
    ("weights", 0, 0, (1, 2)),
    ("weights", 1, 0, (0,)),
    ("keys", 0, 1),
    ("weights", 1, 1, (0, 1, 2)),
    ("weights", 1, 2, (0, 1, 2)),
    ("weights", 1, 0, (1, 2)),
)

WEIGHT_BUFFERS = {1: 4, 2: 1, 3: 3}

PIECES = (
    ((0, 0, 0), "SVVV"),
    ((0, 2, 1), "VVVV"),
    ((0, 2, 2), "SSSS"),
    ((0, 2, 0), "SSSS"),
    ((0, 1, 1), "SSSS"),
    ((0, 1, 0), "VVVV"),
    ((0, 1, 2), "VVVV"),
    ((0, 0, 1), "SSSS"),
    ((1, 0, 0), "SSVV"),
    ((0, 0, 2), "VVVV"),
    ((1, 1, 0), "SSSS"),
    ((1, 2, 0), "VVVV"),
    ((1, 1, 1), "SSSS"),
    ((1, 2, 1), "SSSS"),
    ((1, 0, 1), "SSSS"),
    ((1, 1, 2), "VVVV"),
    ((1, 0, 2), "SSSS"),
    ((1, 2, 2), "SSSS"),
)
LAST_PIECE = (1, 2, 2)

STEPS = (
    (("spread_scale", 0), ("spread_scale", 1), ("spread_scale", 2),),
    (("quantize_weights", 0, 0, 0), ("quantize_weights", 0, 2, 1), ("scale_keys", 0), ("turn_embedding", 0),
     ("turn_embedding", 1), ("turn_embedding", 2), ("quantize_embedding", 1),),
    (("scale_keys", 1), ("scale_keys", 2),),
    (("scale_keys", 3), ("turn_keys", 1, 0, 0), ("turn_keys", 1, 1, 0), ("turn_keys", 1, 1, 1),),
    (("turn_keys", 1, 0, 1), ("quantize_embedding", 0), ("quantize_embedding", 2),),
    (),
    (("quantize_weights", 0, 1, 0), ("quantize_weights", 0, 2, 0), ("quantize_weights", 0, 2, 2),
     ("turn_keys", 0, 2, 0),),
    (("quantize_weights", 0, 1, 1), ("quantize_weights", 0, 1, 2), ("turn_keys", 0, 0, 0),
     ("turn_keys", 0, 1, 0), ("quantize_keys", 1, 0), ("project", 0, 0, 0), ("project", 0, 0, 1),),
    (("add_bias", 0, 0, 0), ("turn_keys", 0, 0, 1), ("turn_keys", 0, 2, 1), ("quantize_keys", 1, 1),),
    (("quantize_weights", 0, 0, 1), ("quantize_weights", 0, 0, 2), ("quantize_weights", 1, 0, 0),
     ("add_bias", 0, 0, 1), ("turn_keys", 0, 1, 1), ("quantize_keys", 0, 2), ("quantize_query", 0, 0, 0),
     ("quantize_query", 0, 0, 1), ("project", 0, 1, 0), ("project", 0, 2, 0), ("project", 0, 2, 1),),
    (("add_bias", 0, 1, 0), ("add_bias", 0, 2, 0), ("quantize_keys", 0, 0),),
    (("quantize_weights", 1, 1, 0), ("quantize_weights", 1, 2, 0), ("score", 0, 0, 1),),
    (("add_bias", 0, 2, 1), ("quantize_keys", 0, 1), ("project", 0, 1, 1), ("project", 1, 0, 1),
     ("score", 0, 0, 0),),
    (("quantize_weights", 1, 1, 1), ("add_bias", 0, 1, 1), ("quantize_query", 0, 2, 0),
     ("quantize_query", 0, 2, 1),),
    (("quantize_query", 0, 1, 0), ("quantize_query", 0, 1, 1), ("project", 1, 0, 0),),
    (("add_bias", 1, 0, 0), ("score", 0, 1, 0),),
    (("quantize_weights", 1, 0, 1), ("quantize_weights", 1, 1, 2), ("quantize_weights", 1, 2, 1),
     ("add_bias", 1, 0, 1), ("score", 0, 1, 1), ("score", 0, 2, 0), ("score", 0, 2, 1), ("row_max", 0, 0),
     ("row_max", 0, 1),),
    (("turn_keys", 1, 2, 1), ("quantize_query", 1, 0, 0), ("quantize_query", 1, 0, 1), ("exponent", 0, 1),),
    (("quantize_weights", 1, 0, 2), ("turn_keys", 1, 2, 0), ("project", 1, 1, 0), ("project", 1, 1, 1),
     ("exponent", 0, 0),),
    (("quantize_last_weights", 0), ("quantize_last_weights", 1), ("add_bias", 1, 1, 0), ("add_bias", 1, 1, 1),
     ("quantize_query", 1, 1, 0), ("project_last", 0, 0), ("project_last", 0, 1),),
    (("add_bias", 1, 2, 0), ("quantize_keys", 1, 2), ("quantize_query", 1, 2, 0), ("project_last", 1, 0),
     ("project_last", 1, 1), ("score", 1, 0, 0), ("score", 1, 0, 1), ("score", 1, 1, 0), ("score", 1, 2, 0),
     ("normalise", 0, 0),),
    (("add_bias", 1, 2, 1), ("quantize_query", 1, 1, 1), ("quantize_query", 1, 2, 1), ("score", 1, 1, 1),
     ("score", 1, 2, 1), ("row_max", 1, 0), ("row_max", 1, 1), ("exponent", 1, 0), ("exponent", 1, 1),
     ("normalise", 0, 1), ("normalise", 1, 0), ("normalise", 1, 1),),
)


def tile_executor_pa_kernel(tc, inst_embed, Wfc, bfc, Wfp, bfp, Kc, Kp_bytes, Kp_scale, out_0, out_1):
    nc = tc.nc
    weights = (Wfc, Wfp)
    outs = (out_0, out_1)

    with ExitStack() as ctx:
        sbuf = ctx.enter_context(tc.tile_pool(name="sbuf", bufs=1))
        psum = ctx.enter_context(tc.psum_pool(name="psum", bufs=1))
        ctx.enter_context(tc.manual_schedule())

        used = {}

        def turn_name(name, count):
            turn = used.get(name, 0)
            used[name] = turn + 1
            return "%s_%d" % (name, turn % count)

        def rotate(shape, dtype, name, count):
            return sbuf.tile(shape, dtype, name=turn_name(name, count), align_bytes=64)

        def bank_of(shape, dtype, name, count):
            return psum.tile(shape, dtype, name=turn_name(name, count))

        def keep(shape, dtype, name):
            return sbuf.tile(shape, dtype, name=name, align_bytes=64)

        scale_col = keep([P, NPASS, 4], F32, "scale_col")
        nc.scalar.dma_start(out=scale_col[:], in_=Kp_scale.rearrange("o (g p t) -> p (o g) t", p=P, t=4))

        ident = keep([P, P], F32, "ident")
        make_identity(nc, ident[:])

        warm_in = keep([P, 1], F32, "warm_in")
        nc.vector.memset(warm_in[:], 0.0)
        warm_out = keep([P, 1], F32, "warm_out")
        nc.scalar.activation(out=warm_out[:], in_=warm_in[:], func=ACT.Exp)

        raw_weights = {}
        raw_keys = {}
        bias = {}
        embedding = keep([P, 2, DIM], BF16, "embedding")

        def load_weights(c, kp, groups):
            rows = weights[c][kp * PASS:(kp + 1) * PASS, :].rearrange("(p j) n -> p j n", j=4)
            n = len(groups)
            tile = rotate([P, 4, n * GROUP], BF16, "weights_%d" % n, WEIGHT_BUFFERS[n])
            nc.sync.dma_start(out=tile[:], in_=rows[:, :, groups[0] * GROUP:(groups[-1] + 1) * GROUP])
            for i, g in enumerate(groups):
                raw_weights[c, kp, g] = tile[:, :, i * GROUP:(i + 1) * GROUP]

        def load_keys(c, half):
            rows = (Kc, Kp_bytes)[c].rearrange("(b p) k -> p b k", p=P)[:, 2 * half:2 * half + 2, :]
            tile = keep([P, 2, DIM], (BF16, U8)[c], ("keys_%d", "key_bytes_%d")[c] % half)
            nc.sync.dma_start(out=tile[:], in_=rows)
            raw_keys[c, half] = tile

        def load_embedding():
            nc.sync.dma_start(out=embedding[:], in_=inst_embed.rearrange("(h p) k -> p h k", p=P))

        def load_biases():
            for c, vector in enumerate((bfc, bfp)):
                bias[c] = keep([P, NGROUP, 4], BF16, "bias_%d" % c)
                nc.sync.dma_start(out=bias[c][:], in_=vector.rearrange("(g p t) -> p g t", p=P, t=4))

        loads = {"weights": load_weights, "keys": load_keys, "embedding": load_embedding, "biases": load_biases}
        for load in LOADS:
            loads[load[0]](*load[1:])

        def copy(out, in_, on_vector):
            if on_vector:
                nc.vector.tensor_copy(out=out, in_=in_)
            else:
                nc.scalar.copy(out=out, in_=in_)

        def quantize(grouped, name, count=0):
            width = grouped.shape[1] // 4
            if count:
                codes = rotate([P, width], U32, name + "_codes", count)
                scales = rotate([P, width], U8, name + "_scales", count)
            else:
                codes = keep([P, width], U32, name + "_codes")
                scales = keep([P, width], U8, name + "_scales")
            nc.vector.quantize_mx(out=codes[:].bitcast(FP8X4), scales=scales[:], in_=grouped)
            return codes, scales

        def turning_bank():
            return bank_of([P, 4, P], F32, "turning", 3)

        grouped_weights = {}
        weight_codes = {}

        def interleave(piece, shares):
            grouped = rotate([P, 4 * GROUP], BF16, "grouped", 5)
            grouped_weights[piece] = grouped
            rows = raw_weights[piece].rearrange("p j (m t) -> p m j t", t=4)
            by_m = grouped[:].rearrange("p (t m j) -> p m j t", t=4, j=4)
            for letter in ("S", "V"):
                if letter in shares:
                    m0 = 32 * shares.index(letter)
                    m1 = m0 + 32 * len([s for s in shares if s == letter])
                    copy(by_m[:, m0:m1], rows[:, m0:m1], letter == "V")

        def quantize_weights(c, kp, g):
            codes, scales = quantize(grouped_weights[c, kp, g][:], "weight", 13)
            for t in range(4):
                cols = slice(t * P, (t + 1) * P)
                weight_codes[(c, kp, g), t] = (codes[:, cols], scales[:, cols])

        def quantize_last_weights(half):
            codes, scales = quantize(grouped_weights[LAST_PIECE][:, 1024 * half:1024 * (half + 1)], "last_weight_%d" % half)
            for i in range(2):
                cols = slice(i * P, (i + 1) * P)
                weight_codes[LAST_PIECE, 2 * half + i] = (codes[:, cols], scales[:, cols])

        grouped_embedding = {}
        embedding_codes = {}

        def turn_embedding(g, on_vector=False):
            bank = turning_bank()
            for h in range(2):
                words = embedding[:, h, :].bitcast(F32)
                for u in range(2):
                    nc.tensor.transpose(bank[:, 2 * h + u, :], words[:, 256 * g + u:256 * (g + 1):2], ident[:])
            grouped_embedding[g] = keep([P, 4 * TOKENS], BF16, "grouped_embedding_%d" % g)
            copy(grouped_embedding[g][:].bitcast(F32).rearrange("p (h r u) -> p h r u", h=2, u=2),
                 bank[:].rearrange("p (h u) r -> p h r u", u=2), on_vector)

        def quantize_embedding(g):
            embedding_codes[g] = quantize(grouped_embedding[g][:], "embedding_%d" % g)

        scale_row = keep([P, DIM], F32, "scale_row")
        scaled_keys = {}
        grouped_keys = {}
        key_codes = {}

        def spread_scale(g, on_vector=False):
            bank = turning_bank()
            for t in range(4):
                nc.tensor.transpose(bank[:, t, :], scale_col[:, g, t:t + 1].to_broadcast([P, P]), ident[:])
            copy(scale_row[:, g * PASS:(g + 1) * PASS].rearrange("p (n t) -> p n t", t=4),
                 bank[:].rearrange("p t n -> p n t"), on_vector)

        def scale_keys(b):
            scaled_keys[b] = keep([P, DIM], BF16, "scaled_keys_%d" % b)
            nc.vector.tensor_tensor(out=scaled_keys[b][:], in0=raw_keys[1, b // 2][:, b % 2, :].bitcast(FP8),
                                    in1=scale_row[:], op=ALU.mult)

        def turn_keys(c, g, half, on_vector=False):
            bank = turning_bank()
            for i in range(2):
                words = (scaled_keys[2 * half + i][:] if c else raw_keys[0, half][:, i, :]).bitcast(F32)
                for u in range(2):
                    nc.tensor.transpose(bank[:, 2 * i + u, :], words[:, 256 * g + u:256 * (g + 1):2], ident[:])
            if (c, g) not in grouped_keys:
                grouped_keys[c, g] = keep([P, 4 * KEYS], BF16, "grouped_keys_%d%d" % (c, g))
            words = grouped_keys[c, g][:, 1024 * half:1024 * (half + 1)].bitcast(F32)
            copy(words.rearrange("p (i r u) -> p i r u", i=2, u=2), bank[:].rearrange("p (i u) r -> p i r u", u=2), on_vector)

        def quantize_keys(c, g):
            key_codes[c, g] = quantize(grouped_keys[c, g][:], "key_%d%d" % (c, g))

        query_bank = {}
        grouped_query = {}
        query_codes = {}

        def project_slots(c, g, h, slots):
            for t in slots:
                for kp in range(NPASS):
                    w_codes, w_scales = weight_codes[(c, kp, g), t]
                    x_codes, x_scales = embedding_codes[kp]
                    nc.tensor.matmul_mx(
                        out=query_bank[c, g, h][:, t, :],
                        lhsT=w_codes.bitcast(FP8X4), lhsT_scale=w_scales,
                        rhs=x_codes[:, h * P:(h + 1) * P].bitcast(FP8X4), rhs_scale=x_scales[:, h * P:(h + 1) * P],
                        start=(kp == 0), stop=(kp == NPASS - 1))

        def project(c, g, h):
            query_bank[c, g, h] = bank_of([P, 4, P], F32, "query", 3)
            project_slots(c, g, h, (0, 1, 2, 3))

        def project_last(h, half):
            c, _, g = LAST_PIECE
            if half == 0:
                query_bank[c, g, h] = bank_of([P, 4, P], F32, "query", 3)
            project_slots(c, g, h, (2 * half, 2 * half + 1))

        def add_bias(c, g, h):
            grouped = rotate([P, P, 4], BF16, "grouped_query", 6)
            nc.vector.tensor_tensor(
                out=grouped[:], in0=query_bank[c, g, h][:].rearrange("p t n -> p n t"),
                in1=bias[c][:, g, :].unsqueeze(1).to_broadcast([P, P, 4]), op=ALU.add)
            grouped_query[c, g, h] = grouped

        def quantize_query(c, g, h):
            query_codes[c, g, h] = quantize(grouped_query[c, g, h][:].rearrange("p n t -> p (n t)"), "query_%d%d%d" % (c, g, h))

        score_bank = {}
        summed = {}
        neg_max = {}
        exponents = {}
        sums = {}

        def score(c, g, h):
            if (c, h) not in summed:
                score_bank[c, h] = psum.tile([P, KEYS], F32, name="score_%d" % h)
                summed[c, h] = 0
            q_codes, q_scales = query_codes[c, g, h]
            k_codes, k_scales = key_codes[c, g]
            nc.tensor.matmul_mx(
                out=score_bank[c, h][:], lhsT=q_codes[:].bitcast(FP8X4), lhsT_scale=q_scales[:],
                rhs=k_codes[:].bitcast(FP8X4), rhs_scale=k_scales[:],
                start=(summed[c, h] == 0), stop=(summed[c, h] == NGROUP - 1))
            summed[c, h] += 1

        def row_max(c, h):
            unused = rotate([P, KEYS], BF16, "unused", 2)
            neg_max[c, h] = keep([P, 1], F32, "neg_max_%d%d" % (c, h))
            nc.vector.tensor_scalar(out=unused[:], in0=score_bank[c, h][:], scalar1=-SCALE, scalar2=None,
                                    op0=ALU.mult, op1=ALU.min, accum_out=neg_max[c, h][:])

        def exponent(c, h):
            exponents[c, h] = keep([P, KEYS], F32, "exponent_%d" % h)
            sums[c, h] = keep([P, 1], F32, "sum_%d%d" % (c, h))
            nc.scalar.activation(out=exponents[c, h][:], in_=score_bank[c, h][:], func=ACT.Exp,
                                 bias=neg_max[c, h][:], scale=SCALE, accum_out=sums[c, h][:])

        def normalise(c, h):
            factor = keep([P, 1], F32, "factor_%d%d" % (c, h))
            nc.vector.reciprocal(out=factor[:], in_=sums[c, h][:])
            result = keep([P, KEYS], F32, "result_%d%d" % (c, h))
            nc.vector.tensor_scalar(out=result[:], in0=exponents[c, h][:], scalar1=factor[:], scalar2=None, op0=ALU.mult)
            nc.sync.dma_start(out=outs[c][h * P:(h + 1) * P, :], in_=result[:])

        jobs = {
            "quantize_weights": quantize_weights, "quantize_last_weights": quantize_last_weights,
            "turn_embedding": turn_embedding, "quantize_embedding": quantize_embedding,
            "spread_scale": spread_scale, "scale_keys": scale_keys, "turn_keys": turn_keys, "quantize_keys": quantize_keys,
            "project": project, "project_last": project_last, "add_bias": add_bias, "quantize_query": quantize_query,
            "score": score, "row_max": row_max, "exponent": exponent, "normalise": normalise,
        }
        for i, step in enumerate(STEPS):
            if i < len(PIECES):
                interleave(*PIECES[i])
            for job in step:
                jobs[job[0]](*job[1:])
